import numpy as np
import ml_dtypes


def mxq(x, axis, fmt="e4m3"):
    dtype, down = {"e4m3": (ml_dtypes.float8_e4m3fn, 7), "e5m2": (ml_dtypes.float8_e5m2, 14)}[fmt]
    v = np.moveaxis(np.asarray(x, np.float32).astype(ml_dtypes.bfloat16).astype(np.float64), axis, -1)
    blocks = v.reshape(v.shape[:-1] + (-1, 32))
    amax = np.abs(blocks).max(-1, keepdims=True)
    byte = np.maximum(np.where(amax > 0, np.frexp(amax)[1] - 1 + 127, 0) - down, 1)
    scale = np.exp2(byte - 127.0)
    codes = (blocks / scale).astype(np.float32).astype(dtype).astype(np.float64)
    return np.moveaxis((codes * scale).reshape(v.shape), -1, axis)


WIDE = False


def mx_kscale(k):
    if not WIDE:
        return np.ones(k)
    levels = np.array([10, -10, 5, -5, 0])
    a = np.random.permutation(np.resize(levels, k // 512 * 4)).reshape(k // 512, 4)
    idx = np.arange(k)
    return np.exp2(a[idx // 512, idx % 128 // 32])


BF16 = ml_dtypes.bfloat16


def bf(x):
    return np.asarray(x, np.float32).astype(BF16)


def f64(x):
    return np.asarray(x).astype(np.float64)


B, T, N, H, G, GH = 32, 4, 32, 512, 9, 3


def sigmoid(v):
    return 1.0 / (1.0 + np.exp(-v))


def setup_inputs():
    s = mx_kscale(H)
    return {"h_new": bf(np.random.standard_normal((B, T, N, H)) * 0.35 * s),
            "c_new": bf(np.random.standard_normal((B, T, N, H)) * 0.8),
            "g_s": bf(np.random.standard_normal((B, T, H)) * s),
            "c_g_s": bf(np.random.standard_normal((B, T, H)) * 0.5),
            "Wg_s": bf(np.random.standard_normal((GH, T, H, H)) * 2.0 / np.sqrt(H) / s[:, None]),
            "Zg_s": bf(np.random.standard_normal((GH, T, H, H)) * 1.0 / np.sqrt(H) / s[:, None]),
            "bg_s": bf(np.random.standard_normal((GH, T, 1, H)) * 0.3)}


def reference(h_new, c_new, g_s, c_g_s, Wg_s, Zg_s, bg_s):
    c_new, c_g_s = f64(c_new), f64(c_g_s)
    hq = mxq(f64(h_new).transpose(1, 0, 2, 3).reshape(T, B * N, H), 2, "e4m3")
    preg = (hq @ mxq(f64(Wg_s), 2, "e4m3")) + f64(bg_s)
    preg = preg.reshape(GH, T, B, N, H).transpose(0, 2, 1, 3, 4)
    zs_part = mxq(f64(g_s).transpose(1, 0, 2), 2, "e4m3") @ mxq(f64(Zg_s), 2, "e4m3")
    zs_part = zs_part.transpose(0, 2, 1, 3)[:, :, :, None]
    f_s, gg_s, o_s = sigmoid(preg + zs_part)
    c_g_s_new = np.mean(f_s * c_new, axis=2) + np.mean(gg_s, axis=2) * c_g_s
    g_s_new = np.mean(o_s, axis=2) * np.tanh(c_g_s_new)
    return g_s_new, c_g_s_new

@@ -1,0 +1,292 @@
+from contextlib import ExitStack
+
+import concourse.mybir as mybir
+from concourse.masks import make_identity
+
+F32 = mybir.dt.float32
+BF16 = mybir.dt.bfloat16
+U32 = mybir.dt.uint32
+U8 = mybir.dt.uint8
+FP8X4 = mybir.dt.float8_e4m3fn_x4
+ACT = mybir.ActivationFunctionType
+ALU = mybir.AluOpType
+
+P = 128
+PACK = 4
+SEQS = 32
+FRAMES = 4
+BONES = 32
+FEAT = 512
+GATES = 3
+F_GATE, GG_GATE, O_GATE = 0, 1, 2
+UNITS = FRAMES * GATES
+FEAT_TILES = FEAT // P
+BONE_ROWS = P // SEQS
+BONE_STEPS = BONES // BONE_ROWS
+WORDS = FEAT // 2
+COLS = BONES * SEQS
+BANK = 512
+HALVES = COLS // BANK
+BANK_BONES = BANK // SEQS
+
+FLOPS = 2 * GATES * FRAMES * FEAT * FEAT * (COLS + SEQS)
+
+
+def tile_st_hmr_pc_t_kernel(tc, h_new, c_new, g_s, c_g_s, Wg_s, Zg_s, bg_s, out_0, out_1):
+    nc = tc.nc
+    with ExitStack() as ctx:
+        const = ctx.enter_context(tc.tile_pool(name="const", bufs=1))
+        frames = ctx.enter_context(tc.tile_pool(name="frames", bufs=2))
+        raws = ctx.enter_context(tc.tile_pool(name="raws", bufs=3))
+        stage = ctx.enter_context(tc.tile_pool(name="stage", bufs=2))
+        frame_ops = ctx.enter_context(tc.tile_pool(name="frame_ops", bufs=2))
+        weight_ops = ctx.enter_context(tc.tile_pool(name="weight_ops", bufs=3))
+        gate_pool = ctx.enter_context(tc.tile_pool(name="gate_pool", bufs=3))
+        mm = ctx.enter_context(tc.psum_pool(name="mm", bufs=4))
+        flip = ctx.enter_context(tc.psum_pool(name="flip", bufs=4))
+        ctx.enter_context(tc.manual_schedule())
+
+        ident_f32 = const.tile([P, P], F32)
+        make_identity(nc, ident_f32[:])
+        ident_bf = const.tile([P, P], BF16)
+        make_identity(nc, ident_bf[:])
+        sort_f32 = const.tile([P, P], F32)
+        nc.vector.tensor_copy(
+            out=sort_f32[:].rearrange("i (r b) -> i r b", r=BONE_ROWS),
+            in_=ident_f32[:].rearrange("i (b r) -> i r b", r=BONE_ROWS),
+        )
+        sort_bf = const.tile([P, P], BF16)
+        nc.vector.tensor_copy(
+            out=sort_bf[:].rearrange("i (r b) -> i r b", r=BONE_ROWS),
+            in_=ident_bf[:].rearrange("i (b r) -> i r b", r=BONE_ROWS),
+        )
+
+        h_raws, c_raws, wz_raws = {}, {}, {}
+        h_ops, wz_ops, gate_tiles = {}, {}, {}
+
+        def load_rows(raw, src, t):
+            for r in range(BONE_ROWS):
+                nc.sync.dma_start(
+                    out=raw[r:P:BONE_ROWS, :],
+                    in_=src[:, t, r * BONE_STEPS : (r + 1) * BONE_STEPS, :].rearrange("b n k -> b (n k)"),
+                )
+
+        def load_h(t):
+            h_raw = frames.tile([P, BONE_STEPS * FEAT], BF16)
+            load_rows(h_raw, h_new, t)
+            h_raws[t] = h_raw
+
+        def load_c(t):
+            c_raw = frames.tile([P, BONE_STEPS * FEAT], BF16)
+            load_rows(c_raw, c_new, t)
+            c_raws[t] = c_raw
+
+        def load_weights(i):
+            t, g = divmod(i, GATES)
+            wz_raw = raws.tile([P, 2, PACK, FEAT], BF16)
+            for m, weights in enumerate((Wg_s, Zg_s)):
+                nc.sync.dma_start(
+                    out=wz_raw[:, m].rearrange("q (u e) w -> q u (e w)", u=2),
+                    in_=weights[g, t].rearrange("(u q e) w -> q u (e w)", u=2, e=2),
+                )
+            wz_raws[i] = wz_raw
+
+        def quantise_weights(i):
+            wz_raw = wz_raws[i]
+            wz_grouped = stage.tile([P, 2, FEAT, PACK], BF16, align_bytes=64)
+            for m in range(2):
+                nc.vector.tensor_copy(
+                    out=wz_grouped[:, m].rearrange("q (c i) j -> q c j i", i=4),
+                    in_=wz_raw[:, m].rearrange("q j (c i) -> q c j i", i=4),
+                )
+            wz_words = weight_ops.tile([P, 2 * FEAT], U32, align_bytes=64)
+            wz_scales = weight_ops.tile([P, 2 * FEAT], U8, align_bytes=64)
+            nc.vector.quantize_mx(
+                out=wz_words[:].bitcast(FP8X4),
+                scales=wz_scales[:],
+                in_=wz_grouped[:].rearrange("q m w j -> q (m w j)"),
+            )
+            wz_ops[i] = (wz_words, wz_scales)
+
+        def quantise_h(t):
+            h_as_words = h_raws[t][:].bitcast(F32)
+            h_grouped = stage.tile([P, COLS * PACK], BF16, align_bytes=64)
+            h_grouped_words = h_grouped[:].bitcast(F32).rearrange("q (n c u) -> q n c u", c=P, u=2)
+            for pair in range(BONE_STEPS // 2):
+                turned = flip.tile([P, 2, 2, P], F32, tag="flip")
+                for a in range(2):
+                    first_word = (2 * pair + a) * WORDS
+                    for u in range(2):
+                        nc.tensor.transpose(
+                            out=turned[:, a, u, :],
+                            in_=h_as_words[:, first_word + u * P : first_word + (u + 1) * P],
+                            identity=sort_f32[:],
+                        )
+                nc.scalar.copy(
+                    out=h_grouped_words[:, 2 * pair : 2 * pair + 2],
+                    in_=turned[:].rearrange("q a u c -> q a c u"),
+                )
+            h_words = frame_ops.tile([P, COLS], U32, align_bytes=64)
+            h_scales = frame_ops.tile([P, COLS], U8, align_bytes=64)
+            nc.vector.quantize_mx(out=h_words[:].bitcast(FP8X4), scales=h_scales[:], in_=h_grouped[:])
+            h_ops[t] = (h_words, h_scales)
+
+        def gate(i):
+            t, g = divmod(i, GATES)
+            wz_words, wz_scales = wz_ops[i]
+            h_words, h_scales = h_ops[t]
+            values = gate_pool.tile([P, BONES, FEAT_TILES, SEQS], F32)
+            c_turned = {}
+            if g == F_GATE:
+                for x in range(FEAT_TILES):
+                    c_t = flip.tile([P, COLS], BF16, tag="flip")
+                    for n in range(BONE_STEPS):
+                        nc.tensor.transpose(
+                            out=c_t[:, n * P : (n + 1) * P],
+                            in_=c_raws[t][:, n * FEAT + x * P : n * FEAT + (x + 1) * P],
+                            identity=sort_bf[:],
+                        )
+                    c_turned[x] = c_t
+            for x in range(FEAT_TILES):
+                w_cols = slice(x * P, (x + 1) * P)
+                z_cols = slice(FEAT + x * P, FEAT + (x + 1) * P)
+                for half in range(HALVES):
+                    h_cols = slice(half * BANK, (half + 1) * BANK)
+                    pre = mm.tile([P, BANK], F32)
+                    nc.tensor.matmul_mx(
+                        out=pre[:],
+                        lhsT=wz_words[:, w_cols].bitcast(FP8X4),
+                        lhsT_scale=wz_scales[:, w_cols],
+                        rhs=h_words[:, h_cols].bitcast(FP8X4),
+                        rhs_scale=h_scales[:, h_cols],
+                        start=True,
+                        stop=False,
+                    )
+                    nc.tensor.matmul_mx(
+                        out=pre[:],
+                        lhsT=wz_words[:, z_cols].bitcast(FP8X4),
+                        lhsT_scale=wz_scales[:, z_cols],
+                        rhs=g_words[:, t, :].bitcast(FP8X4),
+                        rhs_scale=g_scales[:, t, :],
+                        start=False,
+                        stop=True,
+                    )
+                    bias_col = (g * FRAMES + t) * FEAT_TILES + x
+                    nc.scalar.activation(
+                        out=values[:, half * BANK_BONES : (half + 1) * BANK_BONES, x, :],
+                        in_=pre[:].rearrange("p (n b) -> p n b", b=SEQS),
+                        func=ACT.Sigmoid,
+                        bias=bias_cols[:, bias_col : bias_col + 1],
+                        scale=1.0,
+                    )
+                if g == F_GATE:
+                    nc.vector.tensor_tensor(
+                        out=values[:, :, x, :],
+                        in0=values[:, :, x, :],
+                        in1=c_turned[x][:].rearrange("p (n b) -> p n b", b=SEQS),
+                        op=ALU.mult,
+                    )
+            gate_tiles[i] = values
+
+        def fold_bones(i):
+            values = gate_tiles[i]
+            lower = values[:, 0:BANK_BONES].rearrange("p n x b -> p (n x b)")
+            upper = values[:, BANK_BONES:BONES].rearrange("p n x b -> p (n x b)")
+            nc.vector.tensor_tensor(out=lower, in0=lower, in1=upper, op=ALU.add)
+
+        def sum_bones(i):
+            t, g = divmod(i, GATES)
+            values = gate_tiles[i]
+            total = flip.tile([P, P], F32, tag="flip")
+            for n in range(BANK_BONES):
+                nc.tensor.matmul(
+                    out=total[:],
+                    lhsT=values[:, n].rearrange("p x b -> p (x b)"),
+                    rhs=ident_f32[:],
+                    is_transpose=True,
+                    start=(n == 0),
+                    stop=(n == BANK_BONES - 1),
+                )
+            nc.vector.tensor_scalar_mul(out=means[:, g, t, :], in0=total[:], scalar1=1.0 / BONES)
+            if g == GG_GATE:
+                nc.vector.tensor_tensor(out=c_out[:, t, :], in0=means[:, GG_GATE, t, :], in1=cg[:, t, :], op=ALU.mult)
+                nc.vector.tensor_tensor(out=c_out[:, t, :], in0=c_out[:, t, :], in1=means[:, F_GATE, t, :], op=ALU.add)
+
+        bias_rows = const.tile([P, P], BF16)
+        nc.vector.memset(bias_rows[:], 0.0)
+        nc.sync.dma_start(
+            out=bias_rows[0 : UNITS * FEAT_TILES, :],
+            in_=bg_s.rearrange("g t o (x p) -> (g t o x) p", p=P),
+        )
+        g_raw = const.tile([P, FEAT], BF16)
+        nc.sync.dma_start(out=g_raw[:], in_=g_s.rearrange("b t k -> (b t) k"))
+        load_h(0)
+        load_weights(0)
+        load_c(0)
+        load_weights(1)
+        load_weights(2)
+        cg = const.tile([P, FRAMES, P], BF16)
+        for x in range(FEAT_TILES):
+            nc.sync.dma_start(out=cg[x * SEQS : (x + 1) * SEQS], in_=c_g_s[:, :, x * P : (x + 1) * P])
+
+        bias_turned = flip.tile([P, P], BF16, tag="flip")
+        nc.tensor.transpose(out=bias_turned[:], in_=bias_rows[:], identity=ident_bf[:])
+        bias_cols = const.tile([P, UNITS * FEAT_TILES], F32)
+        nc.vector.tensor_copy(out=bias_cols[:], in_=bias_turned[:, 0 : UNITS * FEAT_TILES])
+
+        g_turned = flip.tile([P, 2, P], F32, tag="flip")
+        for u in range(2):
+            nc.tensor.transpose(
+                out=g_turned[:, u, :],
+                in_=g_raw[:].bitcast(F32)[:, u * P : (u + 1) * P],
+                identity=sort_f32[:],
+            )
+        g_words = const.tile([P, FRAMES, BANK], U32, align_bytes=64)
+        g_scales = const.tile([P, FRAMES, BANK], U8, align_bytes=64)
+        for t in range(FRAMES):
+            g_grouped = stage.tile([P, BANK * PACK], BF16, align_bytes=64)
+            nc.scalar.copy(
+                out=g_grouped[:].bitcast(F32).rearrange("q (n b u) -> q n b u", b=SEQS, u=2),
+                in_=g_turned[:, :, t * SEQS : (t + 1) * SEQS]
+                .rearrange("q u b -> q b u")
+                .unsqueeze(1)
+                .to_broadcast([P, BANK_BONES, SEQS, 2]),
+            )
+            nc.vector.quantize_mx(
+                out=g_words[:, t, :].bitcast(FP8X4), scales=g_scales[:, t, :], in_=g_grouped[:]
+            )
+
+        means = const.tile([P, GATES, FRAMES, P], F32)
+        c_out = const.tile([P, FRAMES, P], F32)
+
+        quantise_h(0)
+        quantise_weights(0)
+        quantise_weights(1)
+
+        for i in range(UNITS):
+            t, g = divmod(i, GATES)
+            if g == F_GATE and t + 1 < FRAMES:
+                load_h(t + 1)
+                load_c(t + 1)
+            if i + 3 < UNITS:
+                load_weights(i + 3)
+            if i >= 1:
+                fold_bones(i - 1)
+            gate(i)
+            if i + 2 < UNITS:
+                quantise_weights(i + 2)
+            if i >= 1:
+                sum_bones(i - 1)
+            if g == GG_GATE and t + 1 < FRAMES:
+                quantise_h(t + 1)
+        fold_bones(UNITS - 1)
+        sum_bones(UNITS - 1)
+
+        tanh_c = const.tile([P, FRAMES, P], F32)
+        nc.scalar.activation(out=tanh_c[:], in_=c_out[:], func=ACT.Tanh)
+        g_out = const.tile([P, FRAMES, P], F32)
+        nc.vector.tensor_tensor(out=g_out[:], in0=means[:, O_GATE], in1=tanh_c[:], op=ALU.mult)
+        for x in range(FEAT_TILES):
+            nc.sync.dma_start(out=out_1[:, :, x * P : (x + 1) * P], in_=c_out[x * SEQS : (x + 1) * SEQS])
+        for x in range(FEAT_TILES):
+            nc.sync.dma_start(out=out_0[:, :, x * P : (x + 1) * P], in_=g_out[x * SEQS : (x + 1) * SEQS])

@@ -28,6 +28,8 @@ COLS = BONES * SEQS
 BANK = 512
 HALVES = COLS // BANK
 BANK_BONES = BANK // SEQS
+AHEAD = 2
+SUM_LAG = 2
 
 FLOPS = 2 * GATES * FRAMES * FEAT * FEAT * (COLS + SEQS)
 
@@ -37,11 +39,11 @@ def tile_st_hmr_pc_t_kernel(tc, h_new, c_new, g_s, c_g_s, Wg_s, Zg_s, bg_s, out_
     with ExitStack() as ctx:
         const = ctx.enter_context(tc.tile_pool(name="const", bufs=1))
         frames = ctx.enter_context(tc.tile_pool(name="frames", bufs=2))
-        raws = ctx.enter_context(tc.tile_pool(name="raws", bufs=3))
+        raws = ctx.enter_context(tc.tile_pool(name="raws", bufs=AHEAD + 1))
         stage = ctx.enter_context(tc.tile_pool(name="stage", bufs=2))
         frame_ops = ctx.enter_context(tc.tile_pool(name="frame_ops", bufs=2))
-        weight_ops = ctx.enter_context(tc.tile_pool(name="weight_ops", bufs=3))
-        gate_pool = ctx.enter_context(tc.tile_pool(name="gate_pool", bufs=3))
+        weight_ops = ctx.enter_context(tc.tile_pool(name="weight_ops", bufs=AHEAD + 1))
+        gate_pool = ctx.enter_context(tc.tile_pool(name="gate_pool", bufs=SUM_LAG + 2))
         mm = ctx.enter_context(tc.psum_pool(name="mm", bufs=4))
         flip = ctx.enter_context(tc.psum_pool(name="flip", bufs=4))
         ctx.enter_context(tc.manual_schedule())
@@ -61,8 +63,8 @@ def tile_st_hmr_pc_t_kernel(tc, h_new, c_new, g_s, c_g_s, Wg_s, Zg_s, bg_s, out_
             in_=ident_bf[:].rearrange("i (b r) -> i r b", r=BONE_ROWS),
         )
 
-        h_raws, c_raws, wz_raws = {}, {}, {}
-        h_ops, wz_ops, gate_tiles = {}, {}, {}
+        h_raws, c_raws, wz_raws, wz_groupeds = {}, {}, {}, {}
+        h_ops, wz_ops, gate_tiles, c_turneds = {}, {}, {}, {}
 
         def load_rows(raw, src, t):
             for r in range(BONE_ROWS):
@@ -91,24 +93,26 @@ def tile_st_hmr_pc_t_kernel(tc, h_new, c_new, g_s, c_g_s, Wg_s, Zg_s, bg_s, out_
                 )
             wz_raws[i] = wz_raw
 
+        def regroup_weights(i, m):
+            if m == 0:
+                wz_grouped = stage.tile([P, 2, FEAT, PACK], BF16, align_bytes=64)
+                wz_groupeds[i] = wz_grouped
+            nc.vector.tensor_copy(
+                out=wz_groupeds[i][:, m].rearrange("q (c i) j -> q c j i", i=4),
+                in_=wz_raws[i][:, m].rearrange("q j (c i) -> q c j i", i=4),
+            )
+
         def quantise_weights(i):
-            wz_raw = wz_raws[i]
-            wz_grouped = stage.tile([P, 2, FEAT, PACK], BF16, align_bytes=64)
-            for m in range(2):
-                nc.vector.tensor_copy(
-                    out=wz_grouped[:, m].rearrange("q (c i) j -> q c j i", i=4),
-                    in_=wz_raw[:, m].rearrange("q j (c i) -> q c j i", i=4),
-                )
             wz_words = weight_ops.tile([P, 2 * FEAT], U32, align_bytes=64)
             wz_scales = weight_ops.tile([P, 2 * FEAT], U8, align_bytes=64)
             nc.vector.quantize_mx(
                 out=wz_words[:].bitcast(FP8X4),
                 scales=wz_scales[:],
-                in_=wz_grouped[:].rearrange("q m w j -> q (m w j)"),
+                in_=wz_groupeds[i][:].rearrange("q m w j -> q (m w j)"),
             )
             wz_ops[i] = (wz_words, wz_scales)
 
-        def quantise_h(t):
+        def turn_frame(t):
             h_as_words = h_raws[t][:].bitcast(F32)
             h_grouped = stage.tile([P, COLS * PACK], BF16, align_bytes=64)
             h_grouped_words = h_grouped[:].bitcast(F32).rearrange("q (n c u) -> q n c u", c=P, u=2)
@@ -126,67 +130,83 @@ def tile_st_hmr_pc_t_kernel(tc, h_new, c_new, g_s, c_g_s, Wg_s, Zg_s, bg_s, out_
                     out=h_grouped_words[:, 2 * pair : 2 * pair + 2],
                     in_=turned[:].rearrange("q a u c -> q a c u"),
                 )
+            g_grouped = stage.tile([P, BANK * PACK], BF16, align_bytes=64)
+            nc.scalar.copy(
+                out=g_grouped[:].bitcast(F32).rearrange("q (n b u) -> q n b u", b=SEQS, u=2),
+                in_=g_sorted[:, :, t * SEQS : (t + 1) * SEQS]
+                .rearrange("q u b -> q b u")
+                .unsqueeze(1)
+                .to_broadcast([P, BANK_BONES, SEQS, 2]),
+            )
+            return h_grouped, g_grouped
+
+        def quantise_frame(t, h_grouped, g_grouped):
             h_words = frame_ops.tile([P, COLS], U32, align_bytes=64)
             h_scales = frame_ops.tile([P, COLS], U8, align_bytes=64)
             nc.vector.quantize_mx(out=h_words[:].bitcast(FP8X4), scales=h_scales[:], in_=h_grouped[:])
-            h_ops[t] = (h_words, h_scales)
+            g_words = frame_ops.tile([P, BANK], U32, align_bytes=64)
+            g_scales = frame_ops.tile([P, BANK], U8, align_bytes=64)
+            nc.vector.quantize_mx(out=g_words[:].bitcast(FP8X4), scales=g_scales[:], in_=g_grouped[:])
+            h_ops[t] = (h_words, h_scales, g_words, g_scales)
 
-        def gate(i):
+        def start_gate(i):
             t, g = divmod(i, GATES)
-            wz_words, wz_scales = wz_ops[i]
-            h_words, h_scales = h_ops[t]
             values = gate_pool.tile([P, BONES, FEAT_TILES, SEQS], F32)
-            c_turned = {}
+            gate_tiles[i] = values
             if g == F_GATE:
                 for x in range(FEAT_TILES):
-                    c_t = flip.tile([P, COLS], BF16, tag="flip")
+                    c_turned = flip.tile([P, COLS], BF16, tag="flip")
                     for n in range(BONE_STEPS):
                         nc.tensor.transpose(
-                            out=c_t[:, n * P : (n + 1) * P],
+                            out=c_turned[:, n * P : (n + 1) * P],
                             in_=c_raws[t][:, n * FEAT + x * P : n * FEAT + (x + 1) * P],
                             identity=sort_bf[:],
                         )
-                    c_turned[x] = c_t
-            for x in range(FEAT_TILES):
-                w_cols = slice(x * P, (x + 1) * P)
-                z_cols = slice(FEAT + x * P, FEAT + (x + 1) * P)
-                for half in range(HALVES):
-                    h_cols = slice(half * BANK, (half + 1) * BANK)
-                    pre = mm.tile([P, BANK], F32)
-                    nc.tensor.matmul_mx(
-                        out=pre[:],
-                        lhsT=wz_words[:, w_cols].bitcast(FP8X4),
-                        lhsT_scale=wz_scales[:, w_cols],
-                        rhs=h_words[:, h_cols].bitcast(FP8X4),
-                        rhs_scale=h_scales[:, h_cols],
-                        start=True,
-                        stop=False,
-                    )
-                    nc.tensor.matmul_mx(
-                        out=pre[:],
-                        lhsT=wz_words[:, z_cols].bitcast(FP8X4),
-                        lhsT_scale=wz_scales[:, z_cols],
-                        rhs=g_words[:, t, :].bitcast(FP8X4),
-                        rhs_scale=g_scales[:, t, :],
-                        start=False,
-                        stop=True,
-                    )
-                    bias_col = (g * FRAMES + t) * FEAT_TILES + x
-                    nc.scalar.activation(
-                        out=values[:, half * BANK_BONES : (half + 1) * BANK_BONES, x, :],
-                        in_=pre[:].rearrange("p (n b) -> p n b", b=SEQS),
-                        func=ACT.Sigmoid,
-                        bias=bias_cols[:, bias_col : bias_col + 1],
-                        scale=1.0,
-                    )
-                if g == F_GATE:
-                    nc.vector.tensor_tensor(
-                        out=values[:, :, x, :],
-                        in0=values[:, :, x, :],
-                        in1=c_turned[x][:].rearrange("p (n b) -> p n b", b=SEQS),
-                        op=ALU.mult,
-                    )
-            gate_tiles[i] = values
+                    c_turneds[x] = c_turned
+
+        def gate_tile(i, x):
+            t, g = divmod(i, GATES)
+            wz_words, wz_scales = wz_ops[i]
+            h_words, h_scales, g_words, g_scales = h_ops[t]
+            values = gate_tiles[i]
+            w_cols = slice(x * P, (x + 1) * P)
+            z_cols = slice(FEAT + x * P, FEAT + (x + 1) * P)
+            for half in range(HALVES):
+                h_cols = slice(half * BANK, (half + 1) * BANK)
+                pre = mm.tile([P, BANK], F32)
+                nc.tensor.matmul_mx(
+                    out=pre[:],
+                    lhsT=wz_words[:, w_cols].bitcast(FP8X4),
+                    lhsT_scale=wz_scales[:, w_cols],
+                    rhs=h_words[:, h_cols].bitcast(FP8X4),
+                    rhs_scale=h_scales[:, h_cols],
+                    start=True,
+                    stop=False,
+                )
+                nc.tensor.matmul_mx(
+                    out=pre[:],
+                    lhsT=wz_words[:, z_cols].bitcast(FP8X4),
+                    lhsT_scale=wz_scales[:, z_cols],
+                    rhs=g_words[:].bitcast(FP8X4),
+                    rhs_scale=g_scales[:],
+                    start=False,
+                    stop=True,
+                )
+                bias_col = (g * FRAMES + t) * FEAT_TILES + x
+                nc.scalar.activation(
+                    out=values[:, half * BANK_BONES : (half + 1) * BANK_BONES, x, :],
+                    in_=pre[:].rearrange("p (n b) -> p n b", b=SEQS),
+                    func=ACT.Sigmoid,
+                    bias=bias_cols[:, bias_col : bias_col + 1],
+                    scale=1.0,
+                )
+            if g == F_GATE:
+                nc.vector.tensor_tensor(
+                    out=values[:, :, x, :],
+                    in0=values[:, :, x, :],
+                    in1=c_turneds[x][:].rearrange("p (n b) -> p n b", b=SEQS),
+                    op=ALU.mult,
+                )
 
         def fold_bones(i):
             values = gate_tiles[i]
@@ -207,32 +227,27 @@ def tile_st_hmr_pc_t_kernel(tc, h_new, c_new, g_s, c_g_s, Wg_s, Zg_s, bg_s, out_
                     start=(n == 0),
                     stop=(n == BANK_BONES - 1),
                 )
-            nc.vector.tensor_scalar_mul(out=means[:, g, t, :], in0=total[:], scalar1=1.0 / BONES)
+            nc.scalar.mul(out=means[:, g, t, :], in_=total[:], mul=1.0 / BONES)
             if g == GG_GATE:
                 nc.vector.tensor_tensor(out=c_out[:, t, :], in0=means[:, GG_GATE, t, :], in1=cg[:, t, :], op=ALU.mult)
                 nc.vector.tensor_tensor(out=c_out[:, t, :], in0=c_out[:, t, :], in1=means[:, F_GATE, t, :], op=ALU.add)
 
         bias_rows = const.tile([P, P], BF16)
         nc.vector.memset(bias_rows[:], 0.0)
+        g_raw = const.tile([P, FEAT], BF16)
+        nc.sync.dma_start(out=g_raw[:], in_=g_s.rearrange("b t k -> (b t) k"))
         nc.sync.dma_start(
             out=bias_rows[0 : UNITS * FEAT_TILES, :],
             in_=bg_s.rearrange("g t o (x p) -> (g t o x) p", p=P),
         )
-        g_raw = const.tile([P, FEAT], BF16)
-        nc.sync.dma_start(out=g_raw[:], in_=g_s.rearrange("b t k -> (b t) k"))
         load_h(0)
         load_weights(0)
         load_c(0)
-        load_weights(1)
-        load_weights(2)
+        for i in range(1, AHEAD + 1):
+            load_weights(i)
         cg = const.tile([P, FRAMES, P], BF16)
         for x in range(FEAT_TILES):
             nc.sync.dma_start(out=cg[x * SEQS : (x + 1) * SEQS], in_=c_g_s[:, :, x * P : (x + 1) * P])
-
-        bias_turned = flip.tile([P, P], BF16, tag="flip")
-        nc.tensor.transpose(out=bias_turned[:], in_=bias_rows[:], identity=ident_bf[:])
-        bias_cols = const.tile([P, UNITS * FEAT_TILES], F32)
-        nc.vector.tensor_copy(out=bias_cols[:], in_=bias_turned[:, 0 : UNITS * FEAT_TILES])
 
         g_turned = flip.tile([P, 2, P], F32, tag="flip")
         for u in range(2):
@@ -241,52 +256,58 @@ def tile_st_hmr_pc_t_kernel(tc, h_new, c_new, g_s, c_g_s, Wg_s, Zg_s, bg_s, out_
                 in_=g_raw[:].bitcast(F32)[:, u * P : (u + 1) * P],
                 identity=sort_f32[:],
             )
-        g_words = const.tile([P, FRAMES, BANK], U32, align_bytes=64)
-        g_scales = const.tile([P, FRAMES, BANK], U8, align_bytes=64)
-        for t in range(FRAMES):
-            g_grouped = stage.tile([P, BANK * PACK], BF16, align_bytes=64)
-            nc.scalar.copy(
-                out=g_grouped[:].bitcast(F32).rearrange("q (n b u) -> q n b u", b=SEQS, u=2),
-                in_=g_turned[:, :, t * SEQS : (t + 1) * SEQS]
-                .rearrange("q u b -> q b u")
-                .unsqueeze(1)
-                .to_broadcast([P, BANK_BONES, SEQS, 2]),
-            )
-            nc.vector.quantize_mx(
-                out=g_words[:, t, :].bitcast(FP8X4), scales=g_scales[:, t, :], in_=g_grouped[:]
-            )
+        g_sorted = const.tile([P, 2, P], F32)
+        nc.scalar.copy(out=g_sorted[:], in_=g_turned[:])
+        bias_turned = flip.tile([P, P], BF16, tag="flip")
+        nc.tensor.transpose(out=bias_turned[:], in_=bias_rows[:], identity=ident_bf[:])
+        bias_cols = const.tile([P, UNITS * FEAT_TILES], F32)
+        nc.vector.tensor_copy(out=bias_cols[:], in_=bias_turned[:, 0 : UNITS * FEAT_TILES])
 
         means = const.tile([P, GATES, FRAMES, P], F32)
         c_out = const.tile([P, FRAMES, P], F32)
 
-        quantise_h(0)
+        first_h_grouped, first_g_grouped = turn_frame(0)
+        regroup_weights(0, 0)
+        regroup_weights(0, 1)
+        quantise_frame(0, first_h_grouped, first_g_grouped)
         quantise_weights(0)
-        quantise_weights(1)
+        for i in range(1, AHEAD):
+            regroup_weights(i, 0)
+            regroup_weights(i, 1)
+            quantise_weights(i)
 
         for i in range(UNITS):
             t, g = divmod(i, GATES)
             if g == F_GATE and t + 1 < FRAMES:
                 load_h(t + 1)
                 load_c(t + 1)
-            if i + 3 < UNITS:
-                load_weights(i + 3)
+            if i + AHEAD + 1 < UNITS:
+                load_weights(i + AHEAD + 1)
+            start_gate(i)
             if i >= 1:
                 fold_bones(i - 1)
-            gate(i)
-            if i + 2 < UNITS:
-                quantise_weights(i + 2)
-            if i >= 1:
-                sum_bones(i - 1)
+            for x in range(FEAT_TILES):
+                gate_tile(i, x)
+                if i + AHEAD < UNITS and x < 2:
+                    regroup_weights(i + AHEAD, x)
+                if i + AHEAD < UNITS and x == 2:
+                    quantise_weights(i + AHEAD)
+            if i >= SUM_LAG:
+                sum_bones(i - SUM_LAG)
             if g == GG_GATE and t + 1 < FRAMES:
-                quantise_h(t + 1)
+                next_h_grouped, next_g_grouped = turn_frame(t + 1)
+                quantise_frame(t + 1, next_h_grouped, next_g_grouped)
         fold_bones(UNITS - 1)
-        sum_bones(UNITS - 1)
+        for i in range(UNITS - SUM_LAG, UNITS - 1):
+            sum_bones(i)
 
-        tanh_c = const.tile([P, FRAMES, P], F32)
-        nc.scalar.activation(out=tanh_c[:], in_=c_out[:], func=ACT.Tanh)
-        g_out = const.tile([P, FRAMES, P], F32)
-        nc.vector.tensor_tensor(out=g_out[:], in0=means[:, O_GATE], in1=tanh_c[:], op=ALU.mult)
         for x in range(FEAT_TILES):
             nc.sync.dma_start(out=out_1[:, :, x * P : (x + 1) * P], in_=c_out[x * SEQS : (x + 1) * SEQS])
+        tanh_c = const.tile([P, FRAMES, P], F32)
+        nc.scalar.activation(out=tanh_c[:], in_=c_out[:], func=ACT.Tanh)
+        sum_bones(UNITS - 1)
+        g_out = const.tile([P, FRAMES, P], F32)
+        for t in range(FRAMES):
+            nc.vector.tensor_tensor(out=g_out[:, t, :], in0=means[:, O_GATE, t, :], in1=tanh_c[:, t, :], op=ALU.mult)
         for x in range(FEAT_TILES):
             nc.sync.dma_start(out=out_0[:, :, x * P : (x + 1) * P], in_=g_out[x * SEQS : (x + 1) * SEQS])

@@ -284,12 +284,14 @@ def tile_st_hmr_pc_t_kernel(tc, h_new, c_new, g_s, c_g_s, Wg_s, Zg_s, bg_s, out_
             if i + AHEAD + 1 < UNITS:
                 load_weights(i + AHEAD + 1)
             start_gate(i)
-            if i >= 1:
-                fold_bones(i - 1)
+            if i + AHEAD < UNITS:
+                regroup_weights(i + AHEAD, 0)
             for x in range(FEAT_TILES):
                 gate_tile(i, x)
-                if i + AHEAD < UNITS and x < 2:
-                    regroup_weights(i + AHEAD, x)
+                if i + AHEAD < UNITS and x == 0:
+                    regroup_weights(i + AHEAD, 1)
+                if i >= 1 and x == 1:
+                    fold_bones(i - 1)
                 if i + AHEAD < UNITS and x == 2:
                     quantise_weights(i + AHEAD)
             if i >= SUM_LAG:

@@ -209,6 +209,8 @@ def tile_st_hmr_pc_t_kernel(tc, h_new, c_new, g_s, c_g_s, Wg_s, Zg_s, bg_s, out_
                 )
 
         def fold_bones(i):
+            if i % GATES == O_GATE:
+                return
             values = gate_tiles[i]
             lower = values[:, 0:BANK_BONES].rearrange("p n x b -> p (n x b)")
             upper = values[:, BANK_BONES:BONES].rearrange("p n x b -> p (n x b)")
@@ -218,14 +220,15 @@ def tile_st_hmr_pc_t_kernel(tc, h_new, c_new, g_s, c_g_s, Wg_s, Zg_s, bg_s, out_
             t, g = divmod(i, GATES)
             values = gate_tiles[i]
             total = flip.tile([P, P], F32, tag="flip")
-            for n in range(BANK_BONES):
+            slices = BONES if g == O_GATE else BANK_BONES
+            for n in range(slices):
                 nc.tensor.matmul(
                     out=total[:],
                     lhsT=values[:, n].rearrange("p x b -> p (x b)"),
                     rhs=ident_f32[:],
                     is_transpose=True,
                     start=(n == 0),
-                    stop=(n == BANK_BONES - 1),
+                    stop=(n == slices - 1),
                 )
             nc.scalar.mul(out=means[:, g, t, :], in_=total[:], mul=1.0 / BONES)
             if g == GG_GATE:

from contextlib import ExitStack

import concourse.mybir as mybir
from concourse.masks import make_identity

F32 = mybir.dt.float32
BF16 = mybir.dt.bfloat16
U32 = mybir.dt.uint32
U8 = mybir.dt.uint8
FP8X4 = mybir.dt.float8_e4m3fn_x4
ACT = mybir.ActivationFunctionType
ALU = mybir.AluOpType

P = 128
PACK = 4
SEQS = 32
FRAMES = 4
BONES = 32
FEAT = 512
GATES = 3
F_GATE, GG_GATE, O_GATE = 0, 1, 2
UNITS = FRAMES * GATES
FEAT_TILES = FEAT // P
BONE_ROWS = P // SEQS
BONE_STEPS = BONES // BONE_ROWS
WORDS = FEAT // 2
COLS = BONES * SEQS
BANK = 512
HALVES = COLS // BANK
BANK_BONES = BANK // SEQS
AHEAD = 2
SUM_LAG = 2

FLOPS = 2 * GATES * FRAMES * FEAT * FEAT * (COLS + SEQS)


def tile_st_hmr_pc_t_kernel(tc, h_new, c_new, g_s, c_g_s, Wg_s, Zg_s, bg_s, out_0, out_1):
    nc = tc.nc
    with ExitStack() as ctx:
        const = ctx.enter_context(tc.tile_pool(name="const", bufs=1))
        frames = ctx.enter_context(tc.tile_pool(name="frames", bufs=2))
        raws = ctx.enter_context(tc.tile_pool(name="raws", bufs=AHEAD + 1))
        stage = ctx.enter_context(tc.tile_pool(name="stage", bufs=2))
        frame_ops = ctx.enter_context(tc.tile_pool(name="frame_ops", bufs=2))
        weight_ops = ctx.enter_context(tc.tile_pool(name="weight_ops", bufs=AHEAD + 1))
        gate_pool = ctx.enter_context(tc.tile_pool(name="gate_pool", bufs=SUM_LAG + 2))
        mm = ctx.enter_context(tc.psum_pool(name="mm", bufs=4))
        flip = ctx.enter_context(tc.psum_pool(name="flip", bufs=4))
        ctx.enter_context(tc.manual_schedule())

        ident_f32 = const.tile([P, P], F32)
        make_identity(nc, ident_f32[:])
        ident_bf = const.tile([P, P], BF16)
        make_identity(nc, ident_bf[:])
        sort_f32 = const.tile([P, P], F32)
        nc.vector.tensor_copy(
            out=sort_f32[:].rearrange("i (r b) -> i r b", r=BONE_ROWS),
            in_=ident_f32[:].rearrange("i (b r) -> i r b", r=BONE_ROWS),
        )
        sort_bf = const.tile([P, P], BF16)
        nc.vector.tensor_copy(
            out=sort_bf[:].rearrange("i (r b) -> i r b", r=BONE_ROWS),
            in_=ident_bf[:].rearrange("i (b r) -> i r b", r=BONE_ROWS),
        )

        h_raws, c_raws, wz_raws, wz_groupeds = {}, {}, {}, {}
        h_ops, wz_ops, gate_tiles, c_turneds = {}, {}, {}, {}

        def load_rows(raw, src, t):
            for r in range(BONE_ROWS):
                nc.sync.dma_start(
                    out=raw[r:P:BONE_ROWS, :],
                    in_=src[:, t, r * BONE_STEPS : (r + 1) * BONE_STEPS, :].rearrange("b n k -> b (n k)"),
                )

        def load_h(t):
            h_raw = frames.tile([P, BONE_STEPS * FEAT], BF16)
            load_rows(h_raw, h_new, t)
            h_raws[t] = h_raw

        def load_c(t):
            c_raw = frames.tile([P, BONE_STEPS * FEAT], BF16)
            load_rows(c_raw, c_new, t)
            c_raws[t] = c_raw

        def load_weights(i):
            t, g = divmod(i, GATES)
            wz_raw = raws.tile([P, 2, PACK, FEAT], BF16)
            for m, weights in enumerate((Wg_s, Zg_s)):
                nc.sync.dma_start(
                    out=wz_raw[:, m].rearrange("q (u e) w -> q u (e w)", u=2),
                    in_=weights[g, t].rearrange("(u q e) w -> q u (e w)", u=2, e=2),
                )
            wz_raws[i] = wz_raw

        def regroup_weights(i, m):
            if m == 0:
                wz_grouped = stage.tile([P, 2, FEAT, PACK], BF16, align_bytes=64)
                wz_groupeds[i] = wz_grouped
            nc.vector.tensor_copy(
                out=wz_groupeds[i][:, m].rearrange("q (c i) j -> q c j i", i=4),
                in_=wz_raws[i][:, m].rearrange("q j (c i) -> q c j i", i=4),
            )

        def quantise_weights(i):
            wz_words = weight_ops.tile([P, 2 * FEAT], U32, align_bytes=64)
            wz_scales = weight_ops.tile([P, 2 * FEAT], U8, align_bytes=64)
            nc.vector.quantize_mx(
                out=wz_words[:].bitcast(FP8X4),
                scales=wz_scales[:],
                in_=wz_groupeds[i][:].rearrange("q m w j -> q (m w j)"),
            )
            wz_ops[i] = (wz_words, wz_scales)

        def turn_frame(t):
            h_as_words = h_raws[t][:].bitcast(F32)
            h_grouped = stage.tile([P, COLS * PACK], BF16, align_bytes=64)
            h_grouped_words = h_grouped[:].bitcast(F32).rearrange("q (n c u) -> q n c u", c=P, u=2)
            for pair in range(BONE_STEPS // 2):
                turned = flip.tile([P, 2, 2, P], F32, tag="flip")
                for a in range(2):
                    first_word = (2 * pair + a) * WORDS
                    for u in range(2):
                        nc.tensor.transpose(
                            out=turned[:, a, u, :],
                            in_=h_as_words[:, first_word + u * P : first_word + (u + 1) * P],
                            identity=sort_f32[:],
                        )
                nc.scalar.copy(
                    out=h_grouped_words[:, 2 * pair : 2 * pair + 2],
                    in_=turned[:].rearrange("q a u c -> q a c u"),
                )
            g_grouped = stage.tile([P, BANK * PACK], BF16, align_bytes=64)
            nc.scalar.copy(
                out=g_grouped[:].bitcast(F32).rearrange("q (n b u) -> q n b u", b=SEQS, u=2),
                in_=g_sorted[:, :, t * SEQS : (t + 1) * SEQS]
                .rearrange("q u b -> q b u")
                .unsqueeze(1)
                .to_broadcast([P, BANK_BONES, SEQS, 2]),
            )
            return h_grouped, g_grouped

        def quantise_frame(t, h_grouped, g_grouped):
            h_words = frame_ops.tile([P, COLS], U32, align_bytes=64)
            h_scales = frame_ops.tile([P, COLS], U8, align_bytes=64)
            nc.vector.quantize_mx(out=h_words[:].bitcast(FP8X4), scales=h_scales[:], in_=h_grouped[:])
            g_words = frame_ops.tile([P, BANK], U32, align_bytes=64)
            g_scales = frame_ops.tile([P, BANK], U8, align_bytes=64)
            nc.vector.quantize_mx(out=g_words[:].bitcast(FP8X4), scales=g_scales[:], in_=g_grouped[:])
            h_ops[t] = (h_words, h_scales, g_words, g_scales)

        def start_gate(i):
            t, g = divmod(i, GATES)
            values = gate_pool.tile([P, BONES, FEAT_TILES, SEQS], F32)
            gate_tiles[i] = values
            if g == F_GATE:
                for x in range(FEAT_TILES):
                    c_turned = flip.tile([P, COLS], BF16, tag="flip")
                    for n in range(BONE_STEPS):
                        nc.tensor.transpose(
                            out=c_turned[:, n * P : (n + 1) * P],
                            in_=c_raws[t][:, n * FEAT + x * P : n * FEAT + (x + 1) * P],
                            identity=sort_bf[:],
                        )
                    c_turneds[x] = c_turned

        def gate_tile(i, x):
            t, g = divmod(i, GATES)
            wz_words, wz_scales = wz_ops[i]
            h_words, h_scales, g_words, g_scales = h_ops[t]
            values = gate_tiles[i]
            w_cols = slice(x * P, (x + 1) * P)
            z_cols = slice(FEAT + x * P, FEAT + (x + 1) * P)
            for half in range(HALVES):
                h_cols = slice(half * BANK, (half + 1) * BANK)
                pre = mm.tile([P, BANK], F32)
                nc.tensor.matmul_mx(
                    out=pre[:],
                    lhsT=wz_words[:, w_cols].bitcast(FP8X4),
                    lhsT_scale=wz_scales[:, w_cols],
                    rhs=h_words[:, h_cols].bitcast(FP8X4),
                    rhs_scale=h_scales[:, h_cols],
                    start=True,
                    stop=False,
                )
                nc.tensor.matmul_mx(
                    out=pre[:],
                    lhsT=wz_words[:, z_cols].bitcast(FP8X4),
                    lhsT_scale=wz_scales[:, z_cols],
                    rhs=g_words[:].bitcast(FP8X4),
                    rhs_scale=g_scales[:],
                    start=False,
                    stop=True,
                )
                bias_col = (g * FRAMES + t) * FEAT_TILES + x
                nc.scalar.activation(
                    out=values[:, half * BANK_BONES : (half + 1) * BANK_BONES, x, :],
                    in_=pre[:].rearrange("p (n b) -> p n b", b=SEQS),
                    func=ACT.Sigmoid,
                    bias=bias_cols[:, bias_col : bias_col + 1],
                    scale=1.0,
                )
            if g == F_GATE:
                nc.vector.tensor_tensor(
                    out=values[:, :, x, :],
                    in0=values[:, :, x, :],
                    in1=c_turneds[x][:].rearrange("p (n b) -> p n b", b=SEQS),
                    op=ALU.mult,
                )

        def fold_bones(i):
            if i % GATES == O_GATE:
                return
            values = gate_tiles[i]
            lower = values[:, 0:BANK_BONES].rearrange("p n x b -> p (n x b)")
            upper = values[:, BANK_BONES:BONES].rearrange("p n x b -> p (n x b)")
            nc.vector.tensor_tensor(out=lower, in0=lower, in1=upper, op=ALU.add)

        def sum_bones(i):
            t, g = divmod(i, GATES)
            values = gate_tiles[i]
            total = flip.tile([P, P], F32, tag="flip")
            slices = BONES if g == O_GATE else BANK_BONES
            for n in range(slices):
                nc.tensor.matmul(
                    out=total[:],
                    lhsT=values[:, n].rearrange("p x b -> p (x b)"),
                    rhs=ident_f32[:],
                    is_transpose=True,
                    start=(n == 0),
                    stop=(n == slices - 1),
                )
            nc.scalar.mul(out=means[:, g, t, :], in_=total[:], mul=1.0 / BONES)
            if g == GG_GATE:
                nc.vector.tensor_tensor(out=c_out[:, t, :], in0=means[:, GG_GATE, t, :], in1=cg[:, t, :], op=ALU.mult)
                nc.vector.tensor_tensor(out=c_out[:, t, :], in0=c_out[:, t, :], in1=means[:, F_GATE, t, :], op=ALU.add)

        bias_rows = const.tile([P, P], BF16)
        nc.vector.memset(bias_rows[:], 0.0)
        g_raw = const.tile([P, FEAT], BF16)
        nc.sync.dma_start(out=g_raw[:], in_=g_s.rearrange("b t k -> (b t) k"))
        nc.sync.dma_start(
            out=bias_rows[0 : UNITS * FEAT_TILES, :],
            in_=bg_s.rearrange("g t o (x p) -> (g t o x) p", p=P),
        )
        load_h(0)
        load_weights(0)
        load_c(0)
        for i in range(1, AHEAD + 1):
            load_weights(i)
        cg = const.tile([P, FRAMES, P], BF16)
        for x in range(FEAT_TILES):
            nc.sync.dma_start(out=cg[x * SEQS : (x + 1) * SEQS], in_=c_g_s[:, :, x * P : (x + 1) * P])

        g_turned = flip.tile([P, 2, P], F32, tag="flip")
        for u in range(2):
            nc.tensor.transpose(
                out=g_turned[:, u, :],
                in_=g_raw[:].bitcast(F32)[:, u * P : (u + 1) * P],
                identity=sort_f32[:],
            )
        g_sorted = const.tile([P, 2, P], F32)
        nc.scalar.copy(out=g_sorted[:], in_=g_turned[:])
        bias_turned = flip.tile([P, P], BF16, tag="flip")
        nc.tensor.transpose(out=bias_turned[:], in_=bias_rows[:], identity=ident_bf[:])
        bias_cols = const.tile([P, UNITS * FEAT_TILES], F32)
        nc.vector.tensor_copy(out=bias_cols[:], in_=bias_turned[:, 0 : UNITS * FEAT_TILES])

        means = const.tile([P, GATES, FRAMES, P], F32)
        c_out = const.tile([P, FRAMES, P], F32)

        first_h_grouped, first_g_grouped = turn_frame(0)
        regroup_weights(0, 0)
        regroup_weights(0, 1)
        quantise_frame(0, first_h_grouped, first_g_grouped)
        quantise_weights(0)
        for i in range(1, AHEAD):
            regroup_weights(i, 0)
            regroup_weights(i, 1)
            quantise_weights(i)

        for i in range(UNITS):
            t, g = divmod(i, GATES)
            if g == F_GATE and t + 1 < FRAMES:
                load_h(t + 1)
                load_c(t + 1)
            if i + AHEAD + 1 < UNITS:
                load_weights(i + AHEAD + 1)
            start_gate(i)
            if i + AHEAD < UNITS:
                regroup_weights(i + AHEAD, 0)
            for x in range(FEAT_TILES):
                gate_tile(i, x)
                if i + AHEAD < UNITS and x == 0:
                    regroup_weights(i + AHEAD, 1)
                if i >= 1 and x == 1:
                    fold_bones(i - 1)
                if i + AHEAD < UNITS and x == 2:
                    quantise_weights(i + AHEAD)
            if i >= SUM_LAG:
                sum_bones(i - SUM_LAG)
            if g == GG_GATE and t + 1 < FRAMES:
                next_h_grouped, next_g_grouped = turn_frame(t + 1)
                quantise_frame(t + 1, next_h_grouped, next_g_grouped)
        fold_bones(UNITS - 1)
        for i in range(UNITS - SUM_LAG, UNITS - 1):
            sum_bones(i)

        for x in range(FEAT_TILES):
            nc.sync.dma_start(out=out_1[:, :, x * P : (x + 1) * P], in_=c_out[x * SEQS : (x + 1) * SEQS])
        tanh_c = const.tile([P, FRAMES, P], F32)
        nc.scalar.activation(out=tanh_c[:], in_=c_out[:], func=ACT.Tanh)
        sum_bones(UNITS - 1)
        g_out = const.tile([P, FRAMES, P], F32)
        for t in range(FRAMES):
            nc.vector.tensor_tensor(out=g_out[:, t, :], in0=means[:, O_GATE, t, :], in1=tanh_c[:, t, :], op=ALU.mult)
        for x in range(FEAT_TILES):
            nc.sync.dma_start(out=out_0[:, :, x * P : (x + 1) * P], in_=g_out[x * SEQS : (x + 1) * SEQS])
